import numpy as np
import ml_dtypes


def mxq(x, axis, fmt="e4m3"):
    dtype, down = {"e4m3": (ml_dtypes.float8_e4m3fn, 7), "e5m2": (ml_dtypes.float8_e5m2, 14)}[fmt]
    v = np.moveaxis(np.asarray(x, np.float32).astype(ml_dtypes.bfloat16).astype(np.float64), axis, -1)
    blocks = v.reshape(v.shape[:-1] + (-1, 32))
    amax = np.abs(blocks).max(-1, keepdims=True)
    byte = np.maximum(np.where(amax > 0, np.frexp(amax)[1] - 1 + 127, 0) - down, 1)
    scale = np.exp2(byte - 127.0)
    codes = (blocks / scale).astype(np.float32).astype(dtype).astype(np.float64)
    return np.moveaxis((codes * scale).reshape(v.shape), -1, axis)


WIDE = False


def mx_kscale(k):
    if not WIDE:
        return np.ones(k)
    levels = np.array([10, -10, 5, -5, 0])
    a = np.random.permutation(np.resize(levels, k // 512 * 4)).reshape(k // 512, 4)
    idx = np.arange(k)
    return np.exp2(a[idx // 512, idx % 128 // 32])


BF16 = ml_dtypes.bfloat16


def bf(x):
    return np.asarray(x, np.float32).astype(BF16)


def f64(x):
    return np.asarray(x).astype(np.float64)


B, N, F = 4, 1024, 512
OUT = F


def setup_inputs():
    s = mx_kscale(N)
    adj = np.random.uniform(0.0, 1.0, (N, N))
    adj = adj / adj.sum(axis=1, keepdims=True) * np.sqrt(N)
    return {"prott5_emd": bf(np.random.standard_normal((B, N, F)) / s[None, :, None]),
            "adj": bf(adj * s[None, :]),
            "h0": bf(np.random.standard_normal((B, N, F))),
            "weight": bf(np.random.uniform(-1.0, 1.0, (F, OUT)) * 1.7 / np.sqrt(F)),
            "lamda": 0.5, "alpha": 0.1, "l": 1}


def reference(prott5_emd, adj, h0, weight, lamda, alpha, l):
    theta = min(1.0, np.log(lamda / l + 1.0))
    hi = mxq(f64(adj), 1, "e4m3") @ mxq(f64(prott5_emd), 1, "e4m3")
    support = (1.0 - alpha) * hi + alpha * f64(h0)
    return theta * (mxq(support, 2, "e4m3") @ mxq(f64(weight), 0, "e4m3")) + (1.0 - theta) * support

@@ -1,0 +1,284 @@
+import math
+from contextlib import ExitStack
+
+import concourse.bass as bass
+import concourse.mybir as mybir
+import concourse.tile as tile
+from concourse.masks import make_identity
+
+F32 = mybir.dt.float32
+BF16 = mybir.dt.bfloat16
+U32 = mybir.dt.uint32
+U8 = mybir.dt.uint8
+FP8X4 = mybir.dt.float8_e4m3fn_x4
+MULT = mybir.AluOpType.mult
+ADD = mybir.AluOpType.add
+
+P = 128
+B, N, F = 4, 1024, 512
+R = N // P
+GROUPS = B * R // 2
+FLOPS = 2 * B * N * N * F + 2 * B * N * F * F
+
+PINNED = False
+
+
+def tile_graphconvolution_t_kernel(tc, prott5_emd, adj, h0, weight, lamda, alpha, l, out):
+    nc = tc.nc
+    theta = min(1.0, math.log(lamda / l + 1.0))
+    keep = 1.0 - theta
+    assert keep > 0.0
+    c_hi = keep * (1.0 - alpha)
+    c_h0 = keep * alpha
+
+    with ExitStack() as ctx:
+        const = ctx.enter_context(tc.tile_pool(name="const", bufs=1))
+        agp = ctx.enter_context(tc.tile_pool(name="agp", bufs=2))
+        xgp = ctx.enter_context(tc.tile_pool(name="xgp", bufs=2))
+        hsp = ctx.enter_context(tc.tile_pool(name="hsp", bufs=4))
+        osp = ctx.enter_context(tc.tile_pool(name="osp", bufs=4))
+        sgp = ctx.enter_context(tc.tile_pool(name="sgp", bufs=3))
+        ps_hi = ctx.enter_context(tc.psum_pool(name="ps_hi", bufs=2))
+        ps_tp = ctx.enter_context(tc.psum_pool(name="ps_tp", bufs=4))
+        ps_mm = ctx.enter_context(tc.psum_pool(name="ps_mm", bufs=2))
+        if PINNED:
+            ctx.enter_context(tc.manual_schedule())
+
+        ident = const.tile([P, P], F32, name="ident", tag="ident")
+        adj_raw = const.tile([P, R * N], BF16, name="adj_raw", tag="adj_raw")
+        adj_codes = const.tile([P, R * 256], U32, name="adj_codes", tag="adj_codes", align_bytes=64)
+        adj_scales = const.tile([P, R * 256], U8, name="adj_scales", tag="adj_scales", align_bytes=64)
+        w_raw = const.tile([P, 4 * F], BF16, name="w_raw", tag="w_raw")
+        w_grp = const.tile([P, 4 * F], BF16, name="w_grp", tag="w_grp", align_bytes=64)
+        w_codes = const.tile([P, F], U32, name="w_codes", tag="w_codes", align_bytes=64)
+        w_scales = const.tile([P, F], U8, name="w_scales", tag="w_scales", align_bytes=64)
+        x_raw = [const.tile([P, 8 * F], BF16, name="x_raw%d" % b, tag="x_raw%d" % b) for b in range(B)]
+        h_raw = [const.tile([P, R * F], BF16, name="h_raw%d" % b, tag="h_raw%d" % b) for b in range(B)]
+
+        adj_rows = adj.rearrange("(p r) j -> p (r j)", r=R)
+
+        def load_adj(q):
+            cols = slice(2 * N * q, 2 * N * (q + 1))
+            nc.sync.dma_start(out=adj_raw[:, cols], in_=adj_rows[:, cols])
+
+        def load_x(b, halves):
+            src = prott5_emd[b].rearrange("(a p e) f -> p a (e f)", a=4, e=2)
+            dst = x_raw[b][:].rearrange("p (a x) -> p a x", a=4)
+            for g in halves:
+                nc.sync.dma_start(out=dst[:, 2 * g : 2 * g + 2, :], in_=src[:, 2 * g : 2 * g + 2, :])
+
+        def load_x_whole(b):
+            src = prott5_emd[b].rearrange("(a p e) f -> p a (e f)", a=4, e=2)
+            nc.sync.dma_start(out=x_raw[b][:].rearrange("p (a x) -> p a x", a=4), in_=src)
+
+        def load_h(b, lo, hi_):
+            src = h0[b].rearrange("(p r) f -> p (r f)", r=R)
+            nc.sync.dma_start(out=h_raw[b][:, F * lo : F * hi_], in_=src[:, F * lo : F * hi_])
+
+        load_adj(0)
+        load_x(0, [0, 1])
+        load_h(0, 0, 4)
+        load_adj(1)
+        nc.sync.dma_start(
+            out=w_raw[:].rearrange("p (t o) -> p t o", t=4), in_=weight.rearrange("(t p) o -> p t o", p=P)
+        )
+        load_adj(2)
+        load_adj(3)
+        load_h(0, 4, 8)
+        for b in range(1, B):
+            load_x_whole(b)
+            load_h(b, 0, 8)
+
+        make_identity(nc, ident[:])
+
+        state = {}
+
+        def adj_t(q):
+            for rr in range(2):
+                r = 2 * q + rr
+                xt = ps_tp.tile([P, 512], F32, name="xt", tag="tp")
+                words = adj_raw[:, N * r : N * (r + 1)].bitcast(F32)
+                for j in range(4):
+                    nc.tensor.transpose(xt[:, P * j : P * (j + 1)], words[:, P * j : P * (j + 1)], ident[:])
+                state[("xt", q, rr)] = xt
+
+        def adj_e(q):
+            grp = agp.tile([P, 2048], BF16, name="adj_grp", tag="adj_grp", align_bytes=64)
+            state[("agrp", q)] = grp
+            for rr in range(2):
+                xt = state[("xt", q, rr)]
+                nc.scalar.copy(
+                    out=grp[:].bitcast(F32)[:, 512 * rr : 512 * (rr + 1)].rearrange("p (g i u) -> p g i u", g=2, u=2),
+                    in_=xt[:].rearrange("p (g u i) -> p g i u", g=2, u=2),
+                )
+
+        def adj_q(q):
+            cols = slice(512 * q, 512 * (q + 1))
+            nc.vector.quantize_mx(
+                out=adj_codes[:, cols].bitcast(FP8X4), scales=adj_scales[:, cols], in_=state[("agrp", q)][:]
+            )
+
+        def regroup(engine, dst, src, c0, c1):
+            d = dst.rearrange("p (c i t) -> p c t i", i=4, t=4)[:, c0:c1]
+            s = src.rearrange("p (t c i) -> p c t i", t=4, i=4)[:, c0:c1]
+            if engine == "v":
+                nc.vector.tensor_copy(out=d, in_=s)
+            else:
+                nc.scalar.copy(out=d, in_=s)
+
+        def x_alloc(b):
+            state[("xgrp", b)] = xgp.tile([P, 8 * F], BF16, name="x_grp", tag="x_grp", align_bytes=64)
+            state[("xcod", b)] = xgp.tile([P, 2 * F], U32, name="x_codes", tag="x_codes", align_bytes=64)
+            state[("xsca", b)] = xgp.tile([P, 2 * F], U8, name="x_scales", tag="x_scales", align_bytes=64)
+
+        def x_reg(b, g, half, engine):
+            cols = slice(2048 * g, 2048 * (g + 1))
+            regroup(engine, state[("xgrp", b)][:, cols], x_raw[b][:, cols], 64 * half, 64 * (half + 1))
+
+        def x_q(b, g):
+            nc.vector.quantize_mx(
+                out=state[("xcod", b)][:, F * g : F * (g + 1)].bitcast(FP8X4),
+                scales=state[("xsca", b)][:, F * g : F * (g + 1)],
+                in_=state[("xgrp", b)][:, 2048 * g : 2048 * (g + 1)],
+            )
+
+        def pres(gi):
+            if gi >= GROUPS:
+                return
+            b, q = divmod(gi, 4)
+            hs = hsp.tile([P, 2 * F], F32, name="h0s", tag="h0s")
+            state[("h0s", gi)] = hs
+            nc.scalar.mul(out=hs[:], in_=h_raw[b][:, 2 * F * q : 2 * F * (q + 1)], mul=c_h0)
+
+        def s1(gi):
+            b, q = divmod(gi, 4)
+            for u in range(2):
+                acc = ps_hi.tile([P, F], F32, name="hi", tag="hi")
+                state[("hi", gi, u)] = acc
+                for g in range(2):
+                    a0 = 256 * (2 * q + u) + P * g
+                    nc.tensor.matmul_mx(
+                        out=acc[:],
+                        lhsT=adj_codes[:, a0 : a0 + P].bitcast(FP8X4),
+                        lhsT_scale=adj_scales[:, a0 : a0 + P],
+                        rhs=state[("xcod", b)][:, F * g : F * (g + 1)].bitcast(FP8X4),
+                        rhs_scale=state[("xsca", b)][:, F * g : F * (g + 1)],
+                        start=(g == 0),
+                        stop=(g == 1),
+                    )
+
+        def st_a(gi):
+            if gi % 2 == 0:
+                state[("o", gi // 2)] = osp.tile([P, 4 * F], F32, name="o_sb", tag="o_sb")
+            o = state[("o", gi // 2)]
+            for u in range(2):
+                c0 = F * (2 * (gi % 2) + u)
+                nc.vector.scalar_tensor_tensor(
+                    out=o[:, c0 : c0 + F],
+                    in0=state[("hi", gi, u)][:],
+                    scalar=c_hi,
+                    in1=state[("h0s", gi)][:, F * u : F * (u + 1)],
+                    op0=MULT,
+                    op1=ADD,
+                )
+
+        def st_t(gi):
+            o = state[("o", gi // 2)]
+            for u in range(2):
+                c0 = F * (2 * (gi % 2) + u)
+                tp = ps_tp.tile([P, 512], F32, name="st", tag="tp")
+                state[("st", gi, u)] = tp
+                for c in range(4):
+                    nc.tensor.transpose(tp[:, P * c : P * (c + 1)], o[:, c0 + P * c : c0 + P * (c + 1)], ident[:])
+
+        def st_c(gi):
+            sg = sgp.tile([P, 1024], BF16, name="s_grp", tag="s_grp", align_bytes=64)
+            state[("sg", gi)] = sg
+            for u in range(2):
+                nc.scalar.mul(
+                    out=sg[:, 512 * u : 512 * (u + 1)].rearrange("p (i c) -> p i c", c=4),
+                    in_=state[("st", gi, u)][:].rearrange("p (c i) -> p i c", c=4),
+                    mul=1.0 / keep,
+                )
+
+        def st_q(gi):
+            sc = sgp.tile([P, 256], U32, name="s_codes", tag="s_codes", align_bytes=64)
+            ss = sgp.tile([P, 256], U8, name="s_scales", tag="s_scales", align_bytes=64)
+            state[("sc", gi)] = sc
+            state[("ss", gi)] = ss
+            nc.vector.quantize_mx(out=sc[:].bitcast(FP8X4), scales=ss[:], in_=state[("sg", gi)][:])
+
+        def s2(gi):
+            for u in range(2):
+                mm = ps_mm.tile([P, F], F32, name="mm", tag="mm")
+                state[("mm", gi, u)] = mm
+                nc.tensor.matmul_mx(
+                    out=mm[:],
+                    lhsT=state[("sc", gi)][:, P * u : P * (u + 1)].bitcast(FP8X4),
+                    lhsT_scale=state[("ss", gi)][:, P * u : P * (u + 1)],
+                    rhs=w_codes[:].bitcast(FP8X4),
+                    rhs_scale=w_scales[:],
+                    start=True,
+                    stop=True,
+                )
+
+        def st_e(gi):
+            o = state[("o", gi // 2)]
+            for u in range(2):
+                c0 = F * (2 * (gi % 2) + u)
+                nc.vector.scalar_tensor_tensor(
+                    out=o[:, c0 : c0 + F],
+                    in0=state[("mm", gi, u)][:],
+                    scalar=theta,
+                    in1=o[:, c0 : c0 + F],
+                    op0=MULT,
+                    op1=ADD,
+                )
+            if gi % 2 == 1:
+                b, half = divmod(gi // 2, 2)
+                dst = out[b].rearrange("(p r) o -> p (r o)", r=R)
+                nc.sync.dma_start(out=dst[:, 4 * F * half : 4 * F * (half + 1)], in_=o[:])
+
+        adj_t(0)
+        adj_e(0)
+        x_alloc(0)
+        x_reg(0, 0, 0, "v")
+        x_reg(0, 0, 1, "v")
+        x_reg(0, 1, 0, "v")
+        x_reg(0, 1, 1, "s")
+        adj_q(0)
+        x_q(0, 0)
+        x_q(0, 1)
+        pres(0)
+        pres(1)
+        for k in range(GROUPS + 2):
+            b, ph = divmod(k, 4)
+            if k >= 2:
+                st_q(k - 2)
+            if k < GROUPS:
+                s1(k)
+                st_a(k)
+            if k == 0:
+                regroup("v", w_grp[:], w_raw[:], 0, 128)
+                nc.vector.quantize_mx(out=w_codes[:].bitcast(FP8X4), scales=w_scales[:], in_=w_grp[:])
+            if k >= 2:
+                s2(k - 2)
+                st_e(k - 2)
+            if 1 <= k <= GROUPS:
+                st_t(k - 1)
+            if k < 3:
+                adj_t(k + 1)
+            if 1 <= k <= GROUPS:
+                st_c(k - 1)
+            if k < 3:
+                adj_e(k + 1)
+                adj_q(k + 1)
+            pres(k + 2)
+            if b < B - 1:
+                if ph == 0:
+                    x_alloc(b + 1)
+                x_reg(b + 1, ph // 2, ph % 2, "s")
+                if ph == 1:
+                    x_q(b + 1, 0)
+                if ph == 3:
+                    x_q(b + 1, 1)

@@ -1,9 +1,7 @@
 import math
 from contextlib import ExitStack
 
-import concourse.bass as bass
 import concourse.mybir as mybir
-import concourse.tile as tile
 from concourse.masks import make_identity
 
 F32 = mybir.dt.float32
@@ -20,7 +18,8 @@ R = N // P
 GROUPS = B * R // 2
 FLOPS = 2 * B * N * N * F + 2 * B * N * F * F
 
-PINNED = False
+POOL_PRES = True
+PRES_DVE = ()
 
 
 def tile_graphconvolution_t_kernel(tc, prott5_emd, adj, h0, weight, lamda, alpha, l, out):
@@ -33,16 +32,15 @@ def tile_graphconvolution_t_kernel(tc, prott5_emd, adj, h0, weight, lamda, alpha
 
     with ExitStack() as ctx:
         const = ctx.enter_context(tc.tile_pool(name="const", bufs=1))
-        agp = ctx.enter_context(tc.tile_pool(name="agp", bufs=2))
+        agp = ctx.enter_context(tc.tile_pool(name="agp", bufs=4))
         xgp = ctx.enter_context(tc.tile_pool(name="xgp", bufs=2))
-        hsp = ctx.enter_context(tc.tile_pool(name="hsp", bufs=4))
+        ring = ctx.enter_context(tc.tile_pool(name="ring", bufs=1))
         osp = ctx.enter_context(tc.tile_pool(name="osp", bufs=4))
-        sgp = ctx.enter_context(tc.tile_pool(name="sgp", bufs=3))
+        scp = ctx.enter_context(tc.tile_pool(name="scp", bufs=3))
         ps_hi = ctx.enter_context(tc.psum_pool(name="ps_hi", bufs=2))
         ps_tp = ctx.enter_context(tc.psum_pool(name="ps_tp", bufs=4))
         ps_mm = ctx.enter_context(tc.psum_pool(name="ps_mm", bufs=2))
-        if PINNED:
-            ctx.enter_context(tc.manual_schedule())
+        ctx.enter_context(tc.manual_schedule())
 
         ident = const.tile([P, P], F32, name="ident", tag="ident")
         adj_raw = const.tile([P, R * N], BF16, name="adj_raw", tag="adj_raw")
@@ -61,22 +59,18 @@ def tile_graphconvolution_t_kernel(tc, prott5_emd, adj, h0, weight, lamda, alpha
             cols = slice(2 * N * q, 2 * N * (q + 1))
             nc.sync.dma_start(out=adj_raw[:, cols], in_=adj_rows[:, cols])
 
-        def load_x(b, halves):
+        def load_x(b, a0, a1):
             src = prott5_emd[b].rearrange("(a p e) f -> p a (e f)", a=4, e=2)
             dst = x_raw[b][:].rearrange("p (a x) -> p a x", a=4)
-            for g in halves:
-                nc.sync.dma_start(out=dst[:, 2 * g : 2 * g + 2, :], in_=src[:, 2 * g : 2 * g + 2, :])
-
-        def load_x_whole(b):
-            src = prott5_emd[b].rearrange("(a p e) f -> p a (e f)", a=4, e=2)
-            nc.sync.dma_start(out=x_raw[b][:].rearrange("p (a x) -> p a x", a=4), in_=src)
+            nc.sync.dma_start(out=dst[:, a0:a1, :], in_=src[:, a0:a1, :])
 
         def load_h(b, lo, hi_):
             src = h0[b].rearrange("(p r) f -> p (r f)", r=R)
             nc.sync.dma_start(out=h_raw[b][:, F * lo : F * hi_], in_=src[:, F * lo : F * hi_])
 
         load_adj(0)
-        load_x(0, [0, 1])
+        load_x(0, 0, 2)
+        load_x(0, 2, 4)
         load_h(0, 0, 4)
         load_adj(1)
         nc.sync.dma_start(
@@ -86,31 +80,29 @@ def tile_graphconvolution_t_kernel(tc, prott5_emd, adj, h0, weight, lamda, alpha
         load_adj(3)
         load_h(0, 4, 8)
         for b in range(1, B):
-            load_x_whole(b)
+            load_x(b, 0, 4)
             load_h(b, 0, 8)
 
         make_identity(nc, ident[:])
 
         state = {}
 
-        def adj_t(q):
-            for rr in range(2):
-                r = 2 * q + rr
-                xt = ps_tp.tile([P, 512], F32, name="xt", tag="tp")
-                words = adj_raw[:, N * r : N * (r + 1)].bitcast(F32)
-                for j in range(4):
-                    nc.tensor.transpose(xt[:, P * j : P * (j + 1)], words[:, P * j : P * (j + 1)], ident[:])
-                state[("xt", q, rr)] = xt
+        def adj_t(r):
+            xt = ps_tp.tile([P, 512], F32, name="xt", tag="tp")
+            words = adj_raw[:, N * r : N * (r + 1)].bitcast(F32)
+            for j in range(4):
+                nc.tensor.transpose(xt[:, P * j : P * (j + 1)], words[:, P * j : P * (j + 1)], ident[:])
+            state[("xt", r)] = xt
 
-        def adj_e(q):
-            grp = agp.tile([P, 2048], BF16, name="adj_grp", tag="adj_grp", align_bytes=64)
-            state[("agrp", q)] = grp
-            for rr in range(2):
-                xt = state[("xt", q, rr)]
-                nc.scalar.copy(
-                    out=grp[:].bitcast(F32)[:, 512 * rr : 512 * (rr + 1)].rearrange("p (g i u) -> p g i u", g=2, u=2),
-                    in_=xt[:].rearrange("p (g u i) -> p g i u", g=2, u=2),
-                )
+        def adj_e(r):
+            if r % 2 == 0:
+                state[("agrp", r // 2)] = agp.tile([P, 2048], BF16, name="adj_grp", tag="adj_grp", align_bytes=64)
+            grp = state[("agrp", r // 2)]
+            rr = r % 2
+            nc.scalar.copy(
+                out=grp[:].bitcast(F32)[:, 512 * rr : 512 * (rr + 1)].rearrange("p (g i u) -> p g i u", g=2, u=2),
+                in_=state[("xt", r)][:].rearrange("p (g u i) -> p g i u", g=2, u=2),
+            )
 
         def adj_q(q):
             cols = slice(512 * q, 512 * (q + 1))
@@ -126,29 +118,33 @@ def tile_graphconvolution_t_kernel(tc, prott5_emd, adj, h0, weight, lamda, alpha
             else:
                 nc.scalar.copy(out=d, in_=s)
 
-        def x_alloc(b):
-            state[("xgrp", b)] = xgp.tile([P, 8 * F], BF16, name="x_grp", tag="x_grp", align_bytes=64)
-            state[("xcod", b)] = xgp.tile([P, 2 * F], U32, name="x_codes", tag="x_codes", align_bytes=64)
-            state[("xsca", b)] = xgp.tile([P, 2 * F], U8, name="x_scales", tag="x_scales", align_bytes=64)
-
-        def x_reg(b, g, half, engine):
+        def x_reg(b, g, c0, c1, engine):
+            if ("xgrp", b) not in state:
+                state[("xgrp", b)] = xgp.tile([P, 8 * F], BF16, name="x_grp", tag="x_grp", align_bytes=64)
             cols = slice(2048 * g, 2048 * (g + 1))
-            regroup(engine, state[("xgrp", b)][:, cols], x_raw[b][:, cols], 64 * half, 64 * (half + 1))
+            regroup(engine, state[("xgrp", b)][:, cols], x_raw[b][:, cols], c0, c1)
 
         def x_q(b, g):
+            if g == 0:
+                state[("xcod", b)] = xgp.tile([P, 2 * F], U32, name="x_codes", tag="x_codes", align_bytes=64)
+                state[("xsca", b)] = xgp.tile([P, 2 * F], U8, name="x_scales", tag="x_scales", align_bytes=64)
             nc.vector.quantize_mx(
                 out=state[("xcod", b)][:, F * g : F * (g + 1)].bitcast(FP8X4),
                 scales=state[("xsca", b)][:, F * g : F * (g + 1)],
                 in_=state[("xgrp", b)][:, 2048 * g : 2048 * (g + 1)],
             )
 
-        def pres(gi):
-            if gi >= GROUPS:
-                return
+        def pres(gi, engine):
             b, q = divmod(gi, 4)
-            hs = hsp.tile([P, 2 * F], F32, name="h0s", tag="h0s")
+            hs = ring.tile([P, 2 * F], F32, name="hs%d" % (gi % 3), tag="hs%d" % (gi % 3), offset=4096 * (gi % 3))
             state[("h0s", gi)] = hs
-            nc.scalar.mul(out=hs[:], in_=h_raw[b][:, 2 * F * q : 2 * F * (q + 1)], mul=c_h0)
+            src = h_raw[b][:, 2 * F * q : 2 * F * (q + 1)]
+            if engine == "g":
+                nc.gpsimd.tensor_scalar(out=hs[:], in0=src, scalar1=c_h0, scalar2=0.0, op0=MULT, op1=ADD)
+            elif engine == "v":
+                nc.vector.tensor_scalar_mul(out=hs[:], in0=src, scalar1=c_h0)
+            else:
+                nc.scalar.mul(out=hs[:], in_=src, mul=c_h0)
 
         def s1(gi):
             b, q = divmod(gi, 4)
@@ -167,7 +163,7 @@ def tile_graphconvolution_t_kernel(tc, prott5_emd, adj, h0, weight, lamda, alpha
                         stop=(g == 1),
                     )
 
-        def st_a(gi):
+        def st_a_t(gi):
             if gi % 2 == 0:
                 state[("o", gi // 2)] = osp.tile([P, 4 * F], F32, name="o_sb", tag="o_sb")
             o = state[("o", gi // 2)]
@@ -181,18 +177,15 @@ def tile_graphconvolution_t_kernel(tc, prott5_emd, adj, h0, weight, lamda, alpha
                     op0=MULT,
                     op1=ADD,
                 )
-
-        def st_t(gi):
-            o = state[("o", gi // 2)]
-            for u in range(2):
-                c0 = F * (2 * (gi % 2) + u)
                 tp = ps_tp.tile([P, 512], F32, name="st", tag="tp")
                 state[("st", gi, u)] = tp
                 for c in range(4):
                     nc.tensor.transpose(tp[:, P * c : P * (c + 1)], o[:, c0 + P * c : c0 + P * (c + 1)], ident[:])
 
         def st_c(gi):
-            sg = sgp.tile([P, 1024], BF16, name="s_grp", tag="s_grp", align_bytes=64)
+            sg = ring.tile(
+                [P, 1024], BF16, name="sg%d" % (gi % 3), tag="sg%d" % (gi % 3), align_bytes=64, offset=4096 * (gi % 3)
+            )
             state[("sg", gi)] = sg
             for u in range(2):
                 nc.scalar.mul(
@@ -202,8 +195,8 @@ def tile_graphconvolution_t_kernel(tc, prott5_emd, adj, h0, weight, lamda, alpha
                 )
 
         def st_q(gi):
-            sc = sgp.tile([P, 256], U32, name="s_codes", tag="s_codes", align_bytes=64)
-            ss = sgp.tile([P, 256], U8, name="s_scales", tag="s_scales", align_bytes=64)
+            sc = scp.tile([P, 256], U32, name="s_codes", tag="s_codes", align_bytes=64)
+            ss = scp.tile([P, 256], U8, name="s_scales", tag="s_scales", align_bytes=64)
             state[("sc", gi)] = sc
             state[("ss", gi)] = ss
             nc.vector.quantize_mx(out=sc[:].bitcast(FP8X4), scales=ss[:], in_=state[("sg", gi)][:])
@@ -222,6 +215,13 @@ def tile_graphconvolution_t_kernel(tc, prott5_emd, adj, h0, weight, lamda, alpha
                     stop=True,
                 )
 
+        def store(gi, u0, u1):
+            b, half = divmod(gi // 2, 2)
+            dst = out[b].rearrange("(p r) o -> p (r o)", r=R)
+            nc.sync.dma_start(
+                out=dst[:, F * (4 * half + u0) : F * (4 * half + u1)], in_=state[("o", gi // 2)][:, F * u0 : F * u1]
+            )
+
         def st_e(gi):
             o = state[("o", gi // 2)]
             for u in range(2):
@@ -234,51 +234,78 @@ def tile_graphconvolution_t_kernel(tc, prott5_emd, adj, h0, weight, lamda, alpha
                     op0=MULT,
                     op1=ADD,
                 )
-            if gi % 2 == 1:
-                b, half = divmod(gi // 2, 2)
-                dst = out[b].rearrange("(p r) o -> p (r o)", r=R)
-                nc.sync.dma_start(out=dst[:, 4 * F * half : 4 * F * (half + 1)], in_=o[:])
+                if gi == GROUPS - 1:
+                    if u == 0:
+                        store(gi, 0, 3)
+                    else:
+                        store(gi, 3, 4)
+            if gi % 2 == 1 and gi != GROUPS - 1:
+                store(gi, 0, 4)
+
+        x_chunks = {}
+        x_quants = {}
+        for b in range(1, B):
+            for i in range(4):
+                k = (1, 1, 2, 2)[i] if b == 1 else 4 * b - 5 + i
+                x_chunks[k] = x_chunks.get(k, []) + [(b, i)]
+            x_quants[2 if b == 1 else 4 * b - 3] = (b, 0)
+            x_quants[4 * b - 1] = (b, 1)
 
         adj_t(0)
+        adj_t(1)
         adj_e(0)
-        x_alloc(0)
-        x_reg(0, 0, 0, "v")
-        x_reg(0, 0, 1, "v")
-        x_reg(0, 1, 0, "v")
-        x_reg(0, 1, 1, "s")
+        adj_e(1)
+        x_reg(0, 0, 0, 128, "v")
+        x_reg(0, 1, 0, 64, "v")
+        x_reg(0, 1, 64, 128, "s")
         adj_q(0)
         x_q(0, 0)
         x_q(0, 1)
-        pres(0)
-        pres(1)
+        pres(0, "s")
+        pres(1, "s")
+        s1(0)
+        adj_t(2)
+        adj_t(3)
+
         for k in range(GROUPS + 2):
-            b, ph = divmod(k, 4)
-            if k >= 2:
-                st_q(k - 2)
-            if k < GROUPS:
-                s1(k)
-                st_a(k)
             if k == 0:
+                adj_e(2)
+                adj_e(3)
+            if k < GROUPS:
+                st_a_t(k)
+            if k == 0:
+                for r in range(4, 8):
+                    adj_t(r)
+            if k < GROUPS:
+                st_c(k)
+            if k == 0:
+                for r in range(4, 8):
+                    adj_e(r)
                 regroup("v", w_grp[:], w_raw[:], 0, 128)
+                adj_q(1)
                 nc.vector.quantize_mx(out=w_codes[:].bitcast(FP8X4), scales=w_scales[:], in_=w_grp[:])
+            if k == 1:
+                adj_q(3)
+            if k in x_quants:
+                x_q(x_quants[k][0], x_quants[k][1])
+            if 1 <= k <= GROUPS:
+                st_q(k - 1)
+            if 3 <= k + 2 < GROUPS:
+                if POOL_PRES:
+                    pres(k + 2, "g")
+                elif (k + 2) in PRES_DVE:
+                    pres(k + 2, "v")
             if k >= 2:
-                s2(k - 2)
                 st_e(k - 2)
+            if k == 0:
+                adj_q(2)
+            if k < GROUPS - 1:
+                s1(k + 1)
             if 1 <= k <= GROUPS:
-                st_t(k - 1)
-            if k < 3:
-                adj_t(k + 1)
-            if 1 <= k <= GROUPS:
-                st_c(k - 1)
-            if k < 3:
-                adj_e(k + 1)
-                adj_q(k + 1)
-            pres(k + 2)
-            if b < B - 1:
-                if ph == 0:
-                    x_alloc(b + 1)
-                x_reg(b + 1, ph // 2, ph % 2, "s")
-                if ph == 1:
-                    x_q(b + 1, 0)
-                if ph == 3:
-                    x_q(b + 1, 1)
+                s2(k - 1)
+            if 3 <= k + 2 < GROUPS and not POOL_PRES and (k + 2) not in PRES_DVE:
+                pres(k + 2, "s")
+            for b, i in x_chunks.get(k, []):
+                x_reg(b, i // 2, 64 * (i % 2), 64 * (i % 2) + 64, "s")
+            if k == 0:
+                pres(2, "s")

@@ -18,8 +18,7 @@ R = N // P
 GROUPS = B * R // 2
 FLOPS = 2 * B * N * N * F + 2 * B * N * F * F
 
-POOL_PRES = True
-PRES_DVE = ()
+HOIST_FROM = 5
 
 
 def tile_graphconvolution_t_kernel(tc, prott5_emd, adj, h0, weight, lamda, alpha, l, out):
@@ -37,8 +36,8 @@ def tile_graphconvolution_t_kernel(tc, prott5_emd, adj, h0, weight, lamda, alpha
         ring = ctx.enter_context(tc.tile_pool(name="ring", bufs=1))
         osp = ctx.enter_context(tc.tile_pool(name="osp", bufs=4))
         scp = ctx.enter_context(tc.tile_pool(name="scp", bufs=3))
-        ps_hi = ctx.enter_context(tc.psum_pool(name="ps_hi", bufs=2))
-        ps_tp = ctx.enter_context(tc.psum_pool(name="ps_tp", bufs=4))
+        ps_hi = ctx.enter_context(tc.psum_pool(name="ps_hi", bufs=3))
+        ps_tp = ctx.enter_context(tc.psum_pool(name="ps_tp", bufs=3))
         ps_mm = ctx.enter_context(tc.psum_pool(name="ps_mm", bufs=2))
         ctx.enter_context(tc.manual_schedule())
 
@@ -73,10 +72,10 @@ def tile_graphconvolution_t_kernel(tc, prott5_emd, adj, h0, weight, lamda, alpha
         load_x(0, 2, 4)
         load_h(0, 0, 4)
         load_adj(1)
+        load_adj(2)
         nc.sync.dma_start(
             out=w_raw[:].rearrange("p (t o) -> p t o", t=4), in_=weight.rearrange("(t p) o -> p t o", p=P)
         )
-        load_adj(2)
         load_adj(3)
         load_h(0, 4, 8)
         for b in range(1, B):
@@ -94,15 +93,17 @@ def tile_graphconvolution_t_kernel(tc, prott5_emd, adj, h0, weight, lamda, alpha
                 nc.tensor.transpose(xt[:, P * j : P * (j + 1)], words[:, P * j : P * (j + 1)], ident[:])
             state[("xt", r)] = xt
 
-        def adj_e(r):
+        def adj_e(r, engine):
             if r % 2 == 0:
                 state[("agrp", r // 2)] = agp.tile([P, 2048], BF16, name="adj_grp", tag="adj_grp", align_bytes=64)
             grp = state[("agrp", r // 2)]
             rr = r % 2
-            nc.scalar.copy(
-                out=grp[:].bitcast(F32)[:, 512 * rr : 512 * (rr + 1)].rearrange("p (g i u) -> p g i u", g=2, u=2),
-                in_=state[("xt", r)][:].rearrange("p (g u i) -> p g i u", g=2, u=2),
-            )
+            dst = grp[:].bitcast(F32)[:, 512 * rr : 512 * (rr + 1)].rearrange("p (g i u) -> p g i u", g=2, u=2)
+            src = state[("xt", r)][:].rearrange("p (g u i) -> p g i u", g=2, u=2)
+            if engine == "v":
+                nc.vector.tensor_copy(out=dst, in_=src)
+            else:
+                nc.scalar.copy(out=dst, in_=src)
 
         def adj_q(q):
             cols = slice(512 * q, 512 * (q + 1))
@@ -118,7 +119,8 @@ def tile_graphconvolution_t_kernel(tc, prott5_emd, adj, h0, weight, lamda, alpha
             else:
                 nc.scalar.copy(out=d, in_=s)
 
-        def x_reg(b, g, c0, c1, engine):
+        def x_reg(b, i, engine):
+            g, c0, c1 = i // 2, 64 * (i % 2), 64 * (i % 2) + 64
             if ("xgrp", b) not in state:
                 state[("xgrp", b)] = xgp.tile([P, 8 * F], BF16, name="x_grp", tag="x_grp", align_bytes=64)
             cols = slice(2048 * g, 2048 * (g + 1))
@@ -146,9 +148,9 @@ def tile_graphconvolution_t_kernel(tc, prott5_emd, adj, h0, weight, lamda, alpha
             else:
                 nc.scalar.mul(out=hs[:], in_=src, mul=c_h0)
 
-        def s1(gi):
+        def s1(gi, units):
             b, q = divmod(gi, 4)
-            for u in range(2):
+            for u in units:
                 acc = ps_hi.tile([P, F], F32, name="hi", tag="hi")
                 state[("hi", gi, u)] = acc
                 for g in range(2):
@@ -242,35 +244,38 @@ def tile_graphconvolution_t_kernel(tc, prott5_emd, adj, h0, weight, lamda, alpha
             if gi % 2 == 1 and gi != GROUPS - 1:
                 store(gi, 0, 4)
 
-        x_chunks = {}
-        x_quants = {}
-        for b in range(1, B):
-            for i in range(4):
-                k = (1, 1, 2, 2)[i] if b == 1 else 4 * b - 5 + i
-                x_chunks[k] = x_chunks.get(k, []) + [(b, i)]
-            x_quants[2 if b == 1 else 4 * b - 3] = (b, 0)
-            x_quants[4 * b - 1] = (b, 1)
+        def hoisted(gi):
+            return HOIST_FROM <= gi < GROUPS and gi % 4 != 0
 
         adj_t(0)
         adj_t(1)
-        adj_e(0)
-        adj_e(1)
-        x_reg(0, 0, 0, 128, "v")
-        x_reg(0, 1, 0, 64, "v")
-        x_reg(0, 1, 64, 128, "s")
-        adj_q(0)
-        x_q(0, 0)
-        x_q(0, 1)
+        adj_t(2)
+        adj_e(0, "s")
+        adj_e(1, "s")
+        x_reg(0, 3, "s")
         pres(0, "s")
         pres(1, "s")
-        s1(0)
-        adj_t(2)
+        x_reg(0, 0, "v")
+        x_reg(0, 1, "v")
+        x_q(0, 0)
+        adj_q(0)
+        x_reg(0, 2, "v")
+        x_q(0, 1)
+        s1(0, (0, 1))
         adj_t(3)
 
         for k in range(GROUPS + 2):
             if k == 0:
-                adj_e(2)
-                adj_e(3)
+                adj_e(2, "s")
+                adj_e(3, "s")
+            if k == 1:
+                adj_q(2)
+                x_reg(1, 0, "s")
+                x_reg(1, 1, "s")
+            if k == 2:
+                adj_q(3)
+            if 3 <= k <= 10:
+                x_reg((k + 5) // 4, (k + 5) % 4, "s")
             if k < GROUPS:
                 st_a_t(k)
             if k == 0:
@@ -279,33 +284,34 @@ def tile_graphconvolution_t_kernel(tc, prott5_emd, adj, h0, weight, lamda, alpha
             if k < GROUPS:
                 st_c(k)
             if k == 0:
-                for r in range(4, 8):
-                    adj_e(r)
+                adj_e(4, "s")
+                adj_e(6, "s")
+                pres(2, "s")
+                adj_e(7, "s")
                 regroup("v", w_grp[:], w_raw[:], 0, 128)
-                adj_q(1)
-                nc.vector.quantize_mx(out=w_codes[:].bitcast(FP8X4), scales=w_scales[:], in_=w_grp[:])
             if k == 1:
-                adj_q(3)
-            if k in x_quants:
-                x_q(x_quants[k][0], x_quants[k][1])
+                x_reg(1, 3, "s")
+            if k == 2:
+                x_q(1, 0)
+            if k in (5, 9):
+                x_q((k + 3) // 4, 0)
+            if k in (3, 7, 11):
+                x_q((k + 1) // 4, 1)
             if 1 <= k <= GROUPS:
                 st_q(k - 1)
             if 3 <= k + 2 < GROUPS:
-                if POOL_PRES:
-                    pres(k + 2, "g")
-                elif (k + 2) in PRES_DVE:
-                    pres(k + 2, "v")
+                pres(k + 2, "g")
             if k >= 2:
                 st_e(k - 2)
             if k == 0:
-                adj_q(2)
+                adj_q(1)
+                nc.vector.quantize_mx(out=w_codes[:].bitcast(FP8X4), scales=w_scales[:], in_=w_grp[:])
+                adj_e(5, "v")
+            if k == 1:
+                x_reg(1, 2, "v")
             if k < GROUPS - 1:
-                s1(k + 1)
+                s1(k + 1, (1,) if hoisted(k + 1) else (0, 1))
             if 1 <= k <= GROUPS:
                 s2(k - 1)
-            if 3 <= k + 2 < GROUPS and not POOL_PRES and (k + 2) not in PRES_DVE:
-                pres(k + 2, "s")
-            for b, i in x_chunks.get(k, []):
-                x_reg(b, i // 2, 64 * (i % 2), 64 * (i % 2) + 64, "s")
-            if k == 0:
-                pres(2, "s")
+            if hoisted(k + 2):
+                s1(k + 2, (0,))

@@ -18,8 +18,6 @@ R = N // P
 GROUPS = B * R // 2
 FLOPS = 2 * B * N * N * F + 2 * B * N * F * F
 
-HOIST_FROM = 5
-
 
 def tile_graphconvolution_t_kernel(tc, prott5_emd, adj, h0, weight, lamda, alpha, l, out):
     nc = tc.nc
@@ -54,31 +52,35 @@ def tile_graphconvolution_t_kernel(tc, prott5_emd, adj, h0, weight, lamda, alpha
 
         adj_rows = adj.rearrange("(p r) j -> p (r j)", r=R)
 
-        def load_adj(q):
-            cols = slice(2 * N * q, 2 * N * (q + 1))
-            nc.sync.dma_start(out=adj_raw[:, cols], in_=adj_rows[:, cols])
+        def load_adj(r0, r1):
+            nc.sync.dma_start(out=adj_raw[:, N * r0 : N * r1], in_=adj_rows[:, N * r0 : N * r1])
 
         def load_x(b, a0, a1):
             src = prott5_emd[b].rearrange("(a p e) f -> p a (e f)", a=4, e=2)
             dst = x_raw[b][:].rearrange("p (a x) -> p a x", a=4)
             nc.sync.dma_start(out=dst[:, a0:a1, :], in_=src[:, a0:a1, :])
 
-        def load_h(b, lo, hi_):
+        def load_h(b, r0, r1):
             src = h0[b].rearrange("(p r) f -> p (r f)", r=R)
-            nc.sync.dma_start(out=h_raw[b][:, F * lo : F * hi_], in_=src[:, F * lo : F * hi_])
+            nc.sync.dma_start(out=h_raw[b][:, F * r0 : F * r1], in_=src[:, F * r0 : F * r1])
 
-        load_adj(0)
-        load_x(0, 0, 2)
+        load_adj(0, 1)
         load_x(0, 2, 4)
-        load_h(0, 0, 4)
-        load_adj(1)
-        load_adj(2)
+        load_x(0, 0, 2)
+        load_adj(1, 2)
+        load_adj(2, 4)
+        load_h(0, 0, 2)
+        load_h(0, 2, 4)
         nc.sync.dma_start(
             out=w_raw[:].rearrange("p (t o) -> p t o", t=4), in_=weight.rearrange("(t p) o -> p t o", p=P)
         )
-        load_adj(3)
+        load_adj(4, 6)
+        load_adj(6, 8)
         load_h(0, 4, 8)
-        for b in range(1, B):
+        load_x(1, 0, 2)
+        load_x(1, 2, 4)
+        load_h(1, 0, 8)
+        for b in range(2, B):
             load_x(b, 0, 4)
             load_h(b, 0, 8)
 
@@ -94,7 +96,7 @@ def tile_graphconvolution_t_kernel(tc, prott5_emd, adj, h0, weight, lamda, alpha
             state[("xt", r)] = xt
 
         def adj_e(r, engine):
-            if r % 2 == 0:
+            if ("agrp", r // 2) not in state:
                 state[("agrp", r // 2)] = agp.tile([P, 2048], BF16, name="adj_grp", tag="adj_grp", align_bytes=64)
             grp = state[("agrp", r // 2)]
             rr = r % 2
@@ -105,10 +107,12 @@ def tile_graphconvolution_t_kernel(tc, prott5_emd, adj, h0, weight, lamda, alpha
             else:
                 nc.scalar.copy(out=dst, in_=src)
 
-        def adj_q(q):
-            cols = slice(512 * q, 512 * (q + 1))
+        def adj_q(r0, r1):
+            grp = state[("agrp", r0 // 2)]
             nc.vector.quantize_mx(
-                out=adj_codes[:, cols].bitcast(FP8X4), scales=adj_scales[:, cols], in_=state[("agrp", q)][:]
+                out=adj_codes[:, 256 * r0 : 256 * r1].bitcast(FP8X4),
+                scales=adj_scales[:, 256 * r0 : 256 * r1],
+                in_=grp[:, 1024 * (r0 % 2) : 1024 * (r0 % 2) + 1024 * (r1 - r0)],
             )
 
         def regroup(engine, dst, src, c0, c1):
@@ -237,60 +241,63 @@ def tile_graphconvolution_t_kernel(tc, prott5_emd, adj, h0, weight, lamda, alpha
                     op1=ADD,
                 )
                 if gi == GROUPS - 1:
-                    if u == 0:
-                        store(gi, 0, 3)
-                    else:
-                        store(gi, 3, 4)
-            if gi % 2 == 1 and gi != GROUPS - 1:
+                    store(gi, 2 + u, 3 + u)
+            if gi == GROUPS - 2:
+                store(gi, 0, 2)
+            elif gi % 2 == 1 and gi != GROUPS - 1:
                 store(gi, 0, 4)
 
         def hoisted(gi):
-            return HOIST_FROM <= gi < GROUPS and gi % 4 != 0
+            return 5 <= gi < GROUPS and gi % 4 != 0
 
         adj_t(0)
-        adj_t(1)
-        adj_t(2)
         adj_e(0, "s")
-        adj_e(1, "s")
         x_reg(0, 3, "s")
-        pres(0, "s")
-        pres(1, "s")
-        x_reg(0, 0, "v")
-        x_reg(0, 1, "v")
-        x_q(0, 0)
-        adj_q(0)
         x_reg(0, 2, "v")
+        adj_q(0, 1)
+        x_reg(0, 1, "v")
+        x_reg(0, 0, "v")
+        x_q(0, 0)
         x_q(0, 1)
+        adj_t(1)
+        adj_e(1, "s")
+        adj_q(1, 2)
+        adj_t(2)
+        adj_e(2, "s")
+        pres(1, "s")
+        pres(0, "v")
         s1(0, (0, 1))
         adj_t(3)
 
         for k in range(GROUPS + 2):
             if k == 0:
-                adj_e(2, "s")
                 adj_e(3, "s")
             if k == 1:
-                adj_q(2)
-                x_reg(1, 0, "s")
                 x_reg(1, 1, "s")
-            if k == 2:
-                adj_q(3)
             if 3 <= k <= 10:
                 x_reg((k + 5) // 4, (k + 5) % 4, "s")
             if k < GROUPS:
                 st_a_t(k)
             if k == 0:
-                for r in range(4, 8):
-                    adj_t(r)
+                adj_t(4)
+                adj_t(5)
+                adj_t(6)
             if k < GROUPS:
                 st_c(k)
             if k == 0:
-                adj_e(4, "s")
+                adj_e(5, "s")
                 adj_e(6, "s")
                 pres(2, "s")
-                adj_e(7, "s")
                 regroup("v", w_grp[:], w_raw[:], 0, 128)
+                adj_q(2, 4)
+                nc.vector.quantize_mx(out=w_codes[:].bitcast(FP8X4), scales=w_scales[:], in_=w_grp[:])
+                adj_e(4, "v")
+                adj_q(4, 6)
             if k == 1:
+                x_reg(1, 2, "s")
                 x_reg(1, 3, "s")
+                x_reg(1, 0, "v")
+                adj_q(6, 8)
             if k == 2:
                 x_q(1, 0)
             if k in (5, 9):
@@ -303,15 +310,12 @@ def tile_graphconvolution_t_kernel(tc, prott5_emd, adj, h0, weight, lamda, alpha
                 pres(k + 2, "g")
             if k >= 2:
                 st_e(k - 2)
-            if k == 0:
-                adj_q(1)
-                nc.vector.quantize_mx(out=w_codes[:].bitcast(FP8X4), scales=w_scales[:], in_=w_grp[:])
-                adj_e(5, "v")
-            if k == 1:
-                x_reg(1, 2, "v")
             if k < GROUPS - 1:
                 s1(k + 1, (1,) if hoisted(k + 1) else (0, 1))
             if 1 <= k <= GROUPS:
                 s2(k - 1)
             if hoisted(k + 2):
                 s1(k + 2, (0,))
+            if k == 0:
+                adj_t(7)
+                adj_e(7, "s")

@@ -79,10 +79,12 @@ def tile_graphconvolution_t_kernel(tc, prott5_emd, adj, h0, weight, lamda, alpha
         load_h(0, 4, 8)
         load_x(1, 0, 2)
         load_x(1, 2, 4)
-        load_h(1, 0, 8)
-        for b in range(2, B):
-            load_x(b, 0, 4)
-            load_h(b, 0, 8)
+        load_h(1, 0, 4)
+        load_x(2, 0, 4)
+        load_h(1, 4, 8)
+        load_h(2, 0, 8)
+        load_x(3, 0, 4)
+        load_h(3, 0, 8)
 
         make_identity(nc, ident[:])
 
@@ -200,12 +202,15 @@ def tile_graphconvolution_t_kernel(tc, prott5_emd, adj, h0, weight, lamda, alpha
                     mul=1.0 / keep,
                 )
 
-        def st_q(gi):
-            sc = scp.tile([P, 256], U32, name="s_codes", tag="s_codes", align_bytes=64)
-            ss = scp.tile([P, 256], U8, name="s_scales", tag="s_scales", align_bytes=64)
-            state[("sc", gi)] = sc
-            state[("ss", gi)] = ss
-            nc.vector.quantize_mx(out=sc[:].bitcast(FP8X4), scales=ss[:], in_=state[("sg", gi)][:])
+        def st_q(gi, u0, u1):
+            if ("sc", gi) not in state:
+                state[("sc", gi)] = scp.tile([P, 256], U32, name="s_codes", tag="s_codes", align_bytes=64)
+                state[("ss", gi)] = scp.tile([P, 256], U8, name="s_scales", tag="s_scales", align_bytes=64)
+            nc.vector.quantize_mx(
+                out=state[("sc", gi)][:, P * u0 : P * u1].bitcast(FP8X4),
+                scales=state[("ss", gi)][:, P * u0 : P * u1],
+                in_=state[("sg", gi)][:, 512 * u0 : 512 * u1],
+            )
 
         def s2(gi):
             for u in range(2):
@@ -242,9 +247,11 @@ def tile_graphconvolution_t_kernel(tc, prott5_emd, adj, h0, weight, lamda, alpha
                 )
                 if gi == GROUPS - 1:
                     store(gi, 2 + u, 3 + u)
-            if gi == GROUPS - 2:
-                store(gi, 0, 2)
-            elif gi % 2 == 1 and gi != GROUPS - 1:
+                if gi == GROUPS - 2 and u == 0:
+                    st_q(GROUPS - 1, 1, 2)
+            if GROUPS - 4 <= gi < GROUPS - 1:
+                store(gi, 2 * (gi % 2), 2 * (gi % 2) + 2)
+            elif gi % 2 == 1 and gi < GROUPS - 4:
                 store(gi, 0, 4)
 
         def hoisted(gi):
@@ -274,7 +281,7 @@ def tile_graphconvolution_t_kernel(tc, prott5_emd, adj, h0, weight, lamda, alpha
                 adj_e(3, "s")
             if k == 1:
                 x_reg(1, 1, "s")
-            if 3 <= k <= 10:
+            if 3 <= k <= 10 and k % 4 != 3:
                 x_reg((k + 5) // 4, (k + 5) % 4, "s")
             if k < GROUPS:
                 st_a_t(k)
@@ -284,6 +291,8 @@ def tile_graphconvolution_t_kernel(tc, prott5_emd, adj, h0, weight, lamda, alpha
                 adj_t(6)
             if k < GROUPS:
                 st_c(k)
+            if k in (3, 7):
+                x_reg((k + 5) // 4, 0, "s")
             if k == 0:
                 adj_e(5, "s")
                 adj_e(6, "s")
@@ -304,8 +313,10 @@ def tile_graphconvolution_t_kernel(tc, prott5_emd, adj, h0, weight, lamda, alpha
                 x_q((k + 3) // 4, 0)
             if k in (3, 7, 11):
                 x_q((k + 1) // 4, 1)
-            if 1 <= k <= GROUPS:
-                st_q(k - 1)
+            if 1 <= k < GROUPS:
+                st_q(k - 1, 0, 2)
+            if k == GROUPS:
+                st_q(k - 1, 0, 1)
             if 3 <= k + 2 < GROUPS:
                 pres(k + 2, "g")
             if k >= 2:

@@ -133,7 +133,7 @@ def tile_graphconvolution_t_kernel(tc, prott5_emd, adj, h0, weight, lamda, alpha
             regroup(engine, state[("xgrp", b)][:, cols], x_raw[b][:, cols], c0, c1)
 
         def x_q(b, g):
-            if g == 0:
+            if ("xcod", b) not in state:
                 state[("xcod", b)] = xgp.tile([P, 2 * F], U32, name="x_codes", tag="x_codes", align_bytes=64)
                 state[("xsca", b)] = xgp.tile([P, 2 * F], U8, name="x_scales", tag="x_scales", align_bytes=64)
             nc.vector.quantize_mx(
@@ -159,7 +159,8 @@ def tile_graphconvolution_t_kernel(tc, prott5_emd, adj, h0, weight, lamda, alpha
             for u in units:
                 acc = ps_hi.tile([P, F], F32, name="hi", tag="hi")
                 state[("hi", gi, u)] = acc
-                for g in range(2):
+                halves = (1, 0) if b == 0 else (0, 1)
+                for g in halves:
                     a0 = 256 * (2 * q + u) + P * g
                     nc.tensor.matmul_mx(
                         out=acc[:],
@@ -167,8 +168,8 @@ def tile_graphconvolution_t_kernel(tc, prott5_emd, adj, h0, weight, lamda, alpha
                         lhsT_scale=adj_scales[:, a0 : a0 + P],
                         rhs=state[("xcod", b)][:, F * g : F * (g + 1)].bitcast(FP8X4),
                         rhs_scale=state[("xsca", b)][:, F * g : F * (g + 1)],
-                        start=(g == 0),
-                        stop=(g == 1),
+                        start=(g == halves[0]),
+                        stop=(g == halves[1]),
                     )
 
         def st_a_t(gi):
@@ -264,8 +265,8 @@ def tile_graphconvolution_t_kernel(tc, prott5_emd, adj, h0, weight, lamda, alpha
         adj_q(0, 1)
         x_reg(0, 1, "v")
         x_reg(0, 0, "v")
-        x_q(0, 0)
         x_q(0, 1)
+        x_q(0, 0)
         adj_t(1)
         adj_e(1, "s")
         adj_q(1, 2)
@@ -299,8 +300,8 @@ def tile_graphconvolution_t_kernel(tc, prott5_emd, adj, h0, weight, lamda, alpha
                 pres(2, "s")
                 regroup("v", w_grp[:], w_raw[:], 0, 128)
                 adj_q(2, 4)
-                nc.vector.quantize_mx(out=w_codes[:].bitcast(FP8X4), scales=w_scales[:], in_=w_grp[:])
                 adj_e(4, "v")
+                nc.vector.quantize_mx(out=w_codes[:].bitcast(FP8X4), scales=w_scales[:], in_=w_grp[:])
                 adj_q(4, 6)
             if k == 1:
                 x_reg(1, 2, "s")

@@ -41,12 +41,12 @@ def tile_graphconvolution_t_kernel(tc, prott5_emd, adj, h0, weight, lamda, alpha
 
         ident = const.tile([P, P], F32, name="ident", tag="ident")
         adj_raw = const.tile([P, R * N], BF16, name="adj_raw", tag="adj_raw")
-        adj_codes = const.tile([P, R * 256], U32, name="adj_codes", tag="adj_codes", align_bytes=64)
-        adj_scales = const.tile([P, R * 256], U8, name="adj_scales", tag="adj_scales", align_bytes=64)
+        adj_codes = const.tile([P, R * 256], U32, name="adj_codes", tag="adj_codes", align_bytes=256)
+        adj_scales = const.tile([P, R * 256], U8, name="adj_scales", tag="adj_scales", align_bytes=256)
         w_raw = const.tile([P, 4 * F], BF16, name="w_raw", tag="w_raw")
-        w_grp = const.tile([P, 4 * F], BF16, name="w_grp", tag="w_grp", align_bytes=64)
-        w_codes = const.tile([P, F], U32, name="w_codes", tag="w_codes", align_bytes=64)
-        w_scales = const.tile([P, F], U8, name="w_scales", tag="w_scales", align_bytes=64)
+        w_grp = const.tile([P, 4 * F], BF16, name="w_grp", tag="w_grp", align_bytes=256)
+        w_codes = const.tile([P, F], U32, name="w_codes", tag="w_codes", align_bytes=256)
+        w_scales = const.tile([P, F], U8, name="w_scales", tag="w_scales", align_bytes=256)
         x_raw = [const.tile([P, 8 * F], BF16, name="x_raw%d" % b, tag="x_raw%d" % b) for b in range(B)]
         h_raw = [const.tile([P, R * F], BF16, name="h_raw%d" % b, tag="h_raw%d" % b) for b in range(B)]
 
@@ -99,7 +99,7 @@ def tile_graphconvolution_t_kernel(tc, prott5_emd, adj, h0, weight, lamda, alpha
 
         def adj_e(r, engine):
             if ("agrp", r // 2) not in state:
-                state[("agrp", r // 2)] = agp.tile([P, 2048], BF16, name="adj_grp", tag="adj_grp", align_bytes=64)
+                state[("agrp", r // 2)] = agp.tile([P, 2048], BF16, name="adj_grp", tag="adj_grp", align_bytes=256)
             grp = state[("agrp", r // 2)]
             rr = r % 2
             dst = grp[:].bitcast(F32)[:, 512 * rr : 512 * (rr + 1)].rearrange("p (g i u) -> p g i u", g=2, u=2)
@@ -128,14 +128,14 @@ def tile_graphconvolution_t_kernel(tc, prott5_emd, adj, h0, weight, lamda, alpha
         def x_reg(b, i, engine):
             g, c0, c1 = i // 2, 64 * (i % 2), 64 * (i % 2) + 64
             if ("xgrp", b) not in state:
-                state[("xgrp", b)] = xgp.tile([P, 8 * F], BF16, name="x_grp", tag="x_grp", align_bytes=64)
+                state[("xgrp", b)] = xgp.tile([P, 8 * F], BF16, name="x_grp", tag="x_grp", align_bytes=256)
             cols = slice(2048 * g, 2048 * (g + 1))
             regroup(engine, state[("xgrp", b)][:, cols], x_raw[b][:, cols], c0, c1)
 
         def x_q(b, g):
             if ("xcod", b) not in state:
-                state[("xcod", b)] = xgp.tile([P, 2 * F], U32, name="x_codes", tag="x_codes", align_bytes=64)
-                state[("xsca", b)] = xgp.tile([P, 2 * F], U8, name="x_scales", tag="x_scales", align_bytes=64)
+                state[("xcod", b)] = xgp.tile([P, 2 * F], U32, name="x_codes", tag="x_codes", align_bytes=256)
+                state[("xsca", b)] = xgp.tile([P, 2 * F], U8, name="x_scales", tag="x_scales", align_bytes=256)
             nc.vector.quantize_mx(
                 out=state[("xcod", b)][:, F * g : F * (g + 1)].bitcast(FP8X4),
                 scales=state[("xsca", b)][:, F * g : F * (g + 1)],
@@ -193,7 +193,7 @@ def tile_graphconvolution_t_kernel(tc, prott5_emd, adj, h0, weight, lamda, alpha
 
         def st_c(gi):
             sg = ring.tile(
-                [P, 1024], BF16, name="sg%d" % (gi % 3), tag="sg%d" % (gi % 3), align_bytes=64, offset=4096 * (gi % 3)
+                [P, 1024], BF16, name="sg%d" % (gi % 3), tag="sg%d" % (gi % 3), align_bytes=256, offset=4096 * (gi % 3)
             )
             state[("sg", gi)] = sg
             for u in range(2):
@@ -205,8 +205,8 @@ def tile_graphconvolution_t_kernel(tc, prott5_emd, adj, h0, weight, lamda, alpha
 
         def st_q(gi, u0, u1):
             if ("sc", gi) not in state:
-                state[("sc", gi)] = scp.tile([P, 256], U32, name="s_codes", tag="s_codes", align_bytes=64)
-                state[("ss", gi)] = scp.tile([P, 256], U8, name="s_scales", tag="s_scales", align_bytes=64)
+                state[("sc", gi)] = scp.tile([P, 256], U32, name="s_codes", tag="s_codes", align_bytes=256)
+                state[("ss", gi)] = scp.tile([P, 256], U8, name="s_scales", tag="s_scales", align_bytes=256)
             nc.vector.quantize_mx(
                 out=state[("sc", gi)][:, P * u0 : P * u1].bitcast(FP8X4),
                 scales=state[("ss", gi)][:, P * u0 : P * u1],

@@ -215,7 +215,10 @@ def tile_graphconvolution_t_kernel(tc, prott5_emd, adj, h0, weight, lamda, alpha
 
         def s2(gi):
             for u in range(2):
-                mm = ps_mm.tile([P, F], F32, name="mm", tag="mm")
+                if gi == GROUPS - 2:
+                    mm = ps_hi.tile([P, F], F32, name="mm", tag="hi")
+                else:
+                    mm = ps_mm.tile([P, F], F32, name="mm", tag="mm")
                 state[("mm", gi, u)] = mm
                 nc.tensor.matmul_mx(
                     out=mm[:],
@@ -246,12 +249,12 @@ def tile_graphconvolution_t_kernel(tc, prott5_emd, adj, h0, weight, lamda, alpha
                     op0=MULT,
                     op1=ADD,
                 )
-                if gi == GROUPS - 1:
-                    store(gi, 2 + u, 3 + u)
+                if gi >= GROUPS - 3:
+                    store(gi, 2 * (gi % 2) + u, 2 * (gi % 2) + u + 1)
                 if gi == GROUPS - 2 and u == 0:
                     st_q(GROUPS - 1, 1, 2)
-            if GROUPS - 4 <= gi < GROUPS - 1:
-                store(gi, 2 * (gi % 2), 2 * (gi % 2) + 2)
+            if gi == GROUPS - 4:
+                store(gi, 0, 2)
             elif gi % 2 == 1 and gi < GROUPS - 4:
                 store(gi, 0, 4)
 

@@ -86,9 +86,16 @@ def tile_graphconvolution_t_kernel(tc, prott5_emd, adj, h0, weight, lamda, alpha
         load_x(3, 0, 4)
         load_h(3, 0, 8)
 
+        zeros = const.tile([P, F], BF16, name="zeros", tag="zeros")
+        nc.vector.memset(zeros[:], 0.0)
         make_identity(nc, ident[:])
 
         state = {}
+
+        def warm(count):
+            for i in range(count):
+                spare = ps_mm.tile([P, F], F32, name="mm", tag="mm")
+                nc.tensor.matmul(out=spare[:], lhsT=zeros[:, 0:P], rhs=zeros[:], start=True, stop=True)
 
         def adj_t(r):
             xt = ps_tp.tile([P, 512], F32, name="xt", tag="tp")
@@ -270,6 +277,7 @@ def tile_graphconvolution_t_kernel(tc, prott5_emd, adj, h0, weight, lamda, alpha
         x_reg(0, 0, "v")
         x_q(0, 1)
         x_q(0, 0)
+        warm(3)
         adj_t(1)
         adj_e(1, "s")
         adj_q(1, 2)
@@ -277,6 +285,7 @@ def tile_graphconvolution_t_kernel(tc, prott5_emd, adj, h0, weight, lamda, alpha
         adj_e(2, "s")
         pres(1, "s")
         pres(0, "v")
+        warm(1)
         s1(0, (0, 1))
         adj_t(3)
 
@@ -291,6 +300,7 @@ def tile_graphconvolution_t_kernel(tc, prott5_emd, adj, h0, weight, lamda, alpha
                 st_a_t(k)
             if k == 0:
                 adj_t(4)
+                warm(2)
                 adj_t(5)
                 adj_t(6)
             if k < GROUPS:

import math
from contextlib import ExitStack

import concourse.mybir as mybir
from concourse.masks import make_identity

F32 = mybir.dt.float32
BF16 = mybir.dt.bfloat16
U32 = mybir.dt.uint32
U8 = mybir.dt.uint8
FP8X4 = mybir.dt.float8_e4m3fn_x4
MULT = mybir.AluOpType.mult
ADD = mybir.AluOpType.add

P = 128
B, N, F = 4, 1024, 512
R = N // P
GROUPS = B * R // 2
FLOPS = 2 * B * N * N * F + 2 * B * N * F * F


def tile_graphconvolution_t_kernel(tc, prott5_emd, adj, h0, weight, lamda, alpha, l, out):
    nc = tc.nc
    theta = min(1.0, math.log(lamda / l + 1.0))
    keep = 1.0 - theta
    assert keep > 0.0
    c_hi = keep * (1.0 - alpha)
    c_h0 = keep * alpha

    with ExitStack() as ctx:
        const = ctx.enter_context(tc.tile_pool(name="const", bufs=1))
        agp = ctx.enter_context(tc.tile_pool(name="agp", bufs=4))
        xgp = ctx.enter_context(tc.tile_pool(name="xgp", bufs=2))
        ring = ctx.enter_context(tc.tile_pool(name="ring", bufs=1))
        osp = ctx.enter_context(tc.tile_pool(name="osp", bufs=4))
        scp = ctx.enter_context(tc.tile_pool(name="scp", bufs=3))
        ps_hi = ctx.enter_context(tc.psum_pool(name="ps_hi", bufs=3))
        ps_tp = ctx.enter_context(tc.psum_pool(name="ps_tp", bufs=3))
        ps_mm = ctx.enter_context(tc.psum_pool(name="ps_mm", bufs=2))
        ctx.enter_context(tc.manual_schedule())

        ident = const.tile([P, P], F32, name="ident", tag="ident")
        adj_raw = const.tile([P, R * N], BF16, name="adj_raw", tag="adj_raw")
        adj_codes = const.tile([P, R * 256], U32, name="adj_codes", tag="adj_codes", align_bytes=256)
        adj_scales = const.tile([P, R * 256], U8, name="adj_scales", tag="adj_scales", align_bytes=256)
        w_raw = const.tile([P, 4 * F], BF16, name="w_raw", tag="w_raw")
        w_grp = const.tile([P, 4 * F], BF16, name="w_grp", tag="w_grp", align_bytes=256)
        w_codes = const.tile([P, F], U32, name="w_codes", tag="w_codes", align_bytes=256)
        w_scales = const.tile([P, F], U8, name="w_scales", tag="w_scales", align_bytes=256)
        x_raw = [const.tile([P, 8 * F], BF16, name="x_raw%d" % b, tag="x_raw%d" % b) for b in range(B)]
        h_raw = [const.tile([P, R * F], BF16, name="h_raw%d" % b, tag="h_raw%d" % b) for b in range(B)]

        adj_rows = adj.rearrange("(p r) j -> p (r j)", r=R)

        def load_adj(r0, r1):
            nc.sync.dma_start(out=adj_raw[:, N * r0 : N * r1], in_=adj_rows[:, N * r0 : N * r1])

        def load_x(b, a0, a1):
            src = prott5_emd[b].rearrange("(a p e) f -> p a (e f)", a=4, e=2)
            dst = x_raw[b][:].rearrange("p (a x) -> p a x", a=4)
            nc.sync.dma_start(out=dst[:, a0:a1, :], in_=src[:, a0:a1, :])

        def load_h(b, r0, r1):
            src = h0[b].rearrange("(p r) f -> p (r f)", r=R)
            nc.sync.dma_start(out=h_raw[b][:, F * r0 : F * r1], in_=src[:, F * r0 : F * r1])

        load_adj(0, 1)
        load_x(0, 2, 4)
        load_x(0, 0, 2)
        load_adj(1, 2)
        load_adj(2, 4)
        load_h(0, 0, 2)
        load_h(0, 2, 4)
        nc.sync.dma_start(
            out=w_raw[:].rearrange("p (t o) -> p t o", t=4), in_=weight.rearrange("(t p) o -> p t o", p=P)
        )
        load_adj(4, 6)
        load_adj(6, 8)
        load_h(0, 4, 8)
        load_x(1, 0, 2)
        load_x(1, 2, 4)
        load_h(1, 0, 4)
        load_x(2, 0, 4)
        load_h(1, 4, 8)
        load_h(2, 0, 8)
        load_x(3, 0, 4)
        load_h(3, 0, 8)

        zeros = const.tile([P, F], BF16, name="zeros", tag="zeros")
        nc.vector.memset(zeros[:], 0.0)
        make_identity(nc, ident[:])

        state = {}

        def warm(count):
            for i in range(count):
                spare = ps_mm.tile([P, F], F32, name="mm", tag="mm")
                nc.tensor.matmul(out=spare[:], lhsT=zeros[:, 0:P], rhs=zeros[:], start=True, stop=True)

        def adj_t(r):
            xt = ps_tp.tile([P, 512], F32, name="xt", tag="tp")
            words = adj_raw[:, N * r : N * (r + 1)].bitcast(F32)
            for j in range(4):
                nc.tensor.transpose(xt[:, P * j : P * (j + 1)], words[:, P * j : P * (j + 1)], ident[:])
            state[("xt", r)] = xt

        def adj_e(r, engine):
            if ("agrp", r // 2) not in state:
                state[("agrp", r // 2)] = agp.tile([P, 2048], BF16, name="adj_grp", tag="adj_grp", align_bytes=256)
            grp = state[("agrp", r // 2)]
            rr = r % 2
            dst = grp[:].bitcast(F32)[:, 512 * rr : 512 * (rr + 1)].rearrange("p (g i u) -> p g i u", g=2, u=2)
            src = state[("xt", r)][:].rearrange("p (g u i) -> p g i u", g=2, u=2)
            if engine == "v":
                nc.vector.tensor_copy(out=dst, in_=src)
            else:
                nc.scalar.copy(out=dst, in_=src)

        def adj_q(r0, r1):
            grp = state[("agrp", r0 // 2)]
            nc.vector.quantize_mx(
                out=adj_codes[:, 256 * r0 : 256 * r1].bitcast(FP8X4),
                scales=adj_scales[:, 256 * r0 : 256 * r1],
                in_=grp[:, 1024 * (r0 % 2) : 1024 * (r0 % 2) + 1024 * (r1 - r0)],
            )

        def regroup(engine, dst, src, c0, c1):
            d = dst.rearrange("p (c i t) -> p c t i", i=4, t=4)[:, c0:c1]
            s = src.rearrange("p (t c i) -> p c t i", t=4, i=4)[:, c0:c1]
            if engine == "v":
                nc.vector.tensor_copy(out=d, in_=s)
            else:
                nc.scalar.copy(out=d, in_=s)

        def x_reg(b, i, engine):
            g, c0, c1 = i // 2, 64 * (i % 2), 64 * (i % 2) + 64
            if ("xgrp", b) not in state:
                state[("xgrp", b)] = xgp.tile([P, 8 * F], BF16, name="x_grp", tag="x_grp", align_bytes=256)
            cols = slice(2048 * g, 2048 * (g + 1))
            regroup(engine, state[("xgrp", b)][:, cols], x_raw[b][:, cols], c0, c1)

        def x_q(b, g):
            if ("xcod", b) not in state:
                state[("xcod", b)] = xgp.tile([P, 2 * F], U32, name="x_codes", tag="x_codes", align_bytes=256)
                state[("xsca", b)] = xgp.tile([P, 2 * F], U8, name="x_scales", tag="x_scales", align_bytes=256)
            nc.vector.quantize_mx(
                out=state[("xcod", b)][:, F * g : F * (g + 1)].bitcast(FP8X4),
                scales=state[("xsca", b)][:, F * g : F * (g + 1)],
                in_=state[("xgrp", b)][:, 2048 * g : 2048 * (g + 1)],
            )

        def pres(gi, engine):
            b, q = divmod(gi, 4)
            hs = ring.tile([P, 2 * F], F32, name="hs%d" % (gi % 3), tag="hs%d" % (gi % 3), offset=4096 * (gi % 3))
            state[("h0s", gi)] = hs
            src = h_raw[b][:, 2 * F * q : 2 * F * (q + 1)]
            if engine == "g":
                nc.gpsimd.tensor_scalar(out=hs[:], in0=src, scalar1=c_h0, scalar2=0.0, op0=MULT, op1=ADD)
            elif engine == "v":
                nc.vector.tensor_scalar_mul(out=hs[:], in0=src, scalar1=c_h0)
            else:
                nc.scalar.mul(out=hs[:], in_=src, mul=c_h0)

        def s1(gi, units):
            b, q = divmod(gi, 4)
            for u in units:
                acc = ps_hi.tile([P, F], F32, name="hi", tag="hi")
                state[("hi", gi, u)] = acc
                halves = (1, 0) if b == 0 else (0, 1)
                for g in halves:
                    a0 = 256 * (2 * q + u) + P * g
                    nc.tensor.matmul_mx(
                        out=acc[:],
                        lhsT=adj_codes[:, a0 : a0 + P].bitcast(FP8X4),
                        lhsT_scale=adj_scales[:, a0 : a0 + P],
                        rhs=state[("xcod", b)][:, F * g : F * (g + 1)].bitcast(FP8X4),
                        rhs_scale=state[("xsca", b)][:, F * g : F * (g + 1)],
                        start=(g == halves[0]),
                        stop=(g == halves[1]),
                    )

        def st_a_t(gi):
            if gi % 2 == 0:
                state[("o", gi // 2)] = osp.tile([P, 4 * F], F32, name="o_sb", tag="o_sb")
            o = state[("o", gi // 2)]
            for u in range(2):
                c0 = F * (2 * (gi % 2) + u)
                nc.vector.scalar_tensor_tensor(
                    out=o[:, c0 : c0 + F],
                    in0=state[("hi", gi, u)][:],
                    scalar=c_hi,
                    in1=state[("h0s", gi)][:, F * u : F * (u + 1)],
                    op0=MULT,
                    op1=ADD,
                )
                tp = ps_tp.tile([P, 512], F32, name="st", tag="tp")
                state[("st", gi, u)] = tp
                for c in range(4):
                    nc.tensor.transpose(tp[:, P * c : P * (c + 1)], o[:, c0 + P * c : c0 + P * (c + 1)], ident[:])

        def st_c(gi):
            sg = ring.tile(
                [P, 1024], BF16, name="sg%d" % (gi % 3), tag="sg%d" % (gi % 3), align_bytes=256, offset=4096 * (gi % 3)
            )
            state[("sg", gi)] = sg
            for u in range(2):
                nc.scalar.mul(
                    out=sg[:, 512 * u : 512 * (u + 1)].rearrange("p (i c) -> p i c", c=4),
                    in_=state[("st", gi, u)][:].rearrange("p (c i) -> p i c", c=4),
                    mul=1.0 / keep,
                )

        def st_q(gi, u0, u1):
            if ("sc", gi) not in state:
                state[("sc", gi)] = scp.tile([P, 256], U32, name="s_codes", tag="s_codes", align_bytes=256)
                state[("ss", gi)] = scp.tile([P, 256], U8, name="s_scales", tag="s_scales", align_bytes=256)
            nc.vector.quantize_mx(
                out=state[("sc", gi)][:, P * u0 : P * u1].bitcast(FP8X4),
                scales=state[("ss", gi)][:, P * u0 : P * u1],
                in_=state[("sg", gi)][:, 512 * u0 : 512 * u1],
            )

        def s2(gi):
            for u in range(2):
                if gi == GROUPS - 2:
                    mm = ps_hi.tile([P, F], F32, name="mm", tag="hi")
                else:
                    mm = ps_mm.tile([P, F], F32, name="mm", tag="mm")
                state[("mm", gi, u)] = mm
                nc.tensor.matmul_mx(
                    out=mm[:],
                    lhsT=state[("sc", gi)][:, P * u : P * (u + 1)].bitcast(FP8X4),
                    lhsT_scale=state[("ss", gi)][:, P * u : P * (u + 1)],
                    rhs=w_codes[:].bitcast(FP8X4),
                    rhs_scale=w_scales[:],
                    start=True,
                    stop=True,
                )

        def store(gi, u0, u1):
            b, half = divmod(gi // 2, 2)
            dst = out[b].rearrange("(p r) o -> p (r o)", r=R)
            nc.sync.dma_start(
                out=dst[:, F * (4 * half + u0) : F * (4 * half + u1)], in_=state[("o", gi // 2)][:, F * u0 : F * u1]
            )

        def st_e(gi):
            o = state[("o", gi // 2)]
            for u in range(2):
                c0 = F * (2 * (gi % 2) + u)
                nc.vector.scalar_tensor_tensor(
                    out=o[:, c0 : c0 + F],
                    in0=state[("mm", gi, u)][:],
                    scalar=theta,
                    in1=o[:, c0 : c0 + F],
                    op0=MULT,
                    op1=ADD,
                )
                if gi >= GROUPS - 3:
                    store(gi, 2 * (gi % 2) + u, 2 * (gi % 2) + u + 1)
                if gi == GROUPS - 2 and u == 0:
                    st_q(GROUPS - 1, 1, 2)
            if gi == GROUPS - 4:
                store(gi, 0, 2)
            elif gi % 2 == 1 and gi < GROUPS - 4:
                store(gi, 0, 4)

        def hoisted(gi):
            return 5 <= gi < GROUPS and gi % 4 != 0

        adj_t(0)
        adj_e(0, "s")
        x_reg(0, 3, "s")
        x_reg(0, 2, "v")
        adj_q(0, 1)
        x_reg(0, 1, "v")
        x_reg(0, 0, "v")
        x_q(0, 1)
        x_q(0, 0)
        warm(3)
        adj_t(1)
        adj_e(1, "s")
        adj_q(1, 2)
        adj_t(2)
        adj_e(2, "s")
        pres(1, "s")
        pres(0, "v")
        warm(1)
        s1(0, (0, 1))
        adj_t(3)

        for k in range(GROUPS + 2):
            if k == 0:
                adj_e(3, "s")
            if k == 1:
                x_reg(1, 1, "s")
            if 3 <= k <= 10 and k % 4 != 3:
                x_reg((k + 5) // 4, (k + 5) % 4, "s")
            if k < GROUPS:
                st_a_t(k)
            if k == 0:
                adj_t(4)
                warm(2)
                adj_t(5)
                adj_t(6)
            if k < GROUPS:
                st_c(k)
            if k in (3, 7):
                x_reg((k + 5) // 4, 0, "s")
            if k == 0:
                adj_e(5, "s")
                adj_e(6, "s")
                pres(2, "s")
                regroup("v", w_grp[:], w_raw[:], 0, 128)
                adj_q(2, 4)
                adj_e(4, "v")
                nc.vector.quantize_mx(out=w_codes[:].bitcast(FP8X4), scales=w_scales[:], in_=w_grp[:])
                adj_q(4, 6)
            if k == 1:
                x_reg(1, 2, "s")
                x_reg(1, 3, "s")
                x_reg(1, 0, "v")
                adj_q(6, 8)
            if k == 2:
                x_q(1, 0)
            if k in (5, 9):
                x_q((k + 3) // 4, 0)
            if k in (3, 7, 11):
                x_q((k + 1) // 4, 1)
            if 1 <= k < GROUPS:
                st_q(k - 1, 0, 2)
            if k == GROUPS:
                st_q(k - 1, 0, 1)
            if 3 <= k + 2 < GROUPS:
                pres(k + 2, "g")
            if k >= 2:
                st_e(k - 2)
            if k < GROUPS - 1:
                s1(k + 1, (1,) if hoisted(k + 1) else (0, 1))
            if 1 <= k <= GROUPS:
                s2(k - 1)
            if hoisted(k + 2):
                s1(k + 2, (0,))
            if k == 0:
                adj_t(7)
                adj_e(7, "s")
